import numpy as np
import ml_dtypes


def mxq(x, axis, fmt="e4m3"):
    dtype, down = {"e4m3": (ml_dtypes.float8_e4m3fn, 7), "e5m2": (ml_dtypes.float8_e5m2, 14)}[fmt]
    v = np.moveaxis(np.asarray(x, np.float32).astype(ml_dtypes.bfloat16).astype(np.float64), axis, -1)
    blocks = v.reshape(v.shape[:-1] + (-1, 32))
    amax = np.abs(blocks).max(-1, keepdims=True)
    byte = np.maximum(np.where(amax > 0, np.frexp(amax)[1] - 1 + 127, 0) - down, 1)
    scale = np.exp2(byte - 127.0)
    codes = (blocks / scale).astype(np.float32).astype(dtype).astype(np.float64)
    return np.moveaxis((codes * scale).reshape(v.shape), -1, axis)


WIDE = False


def mx_kscale(k):
    if not WIDE:
        return np.ones(k)
    levels = np.array([10, -10, 5, -5, 0])
    a = np.random.permutation(np.resize(levels, k // 512 * 4)).reshape(k // 512, 4)
    idx = np.arange(k)
    return np.exp2(a[idx // 512, idx % 128 // 32])


BF16 = ml_dtypes.bfloat16


def bf(x):
    return np.asarray(x, np.float32).astype(BF16)


def f64(x):
    return np.asarray(x).astype(np.float64)


B, S, HID, NH, DH = 4, 1024, 1024, 4, 64
DQ = NH * DH


def setup_inputs():
    s = mx_kscale(HID)

    def w():
        return bf(np.random.standard_normal((HID, DQ)) / np.sqrt(HID) / s[:, None])

    def b():
        return bf(np.random.standard_normal(DQ) * 0.3)

    return {"x": bf(np.random.standard_normal((B, S, HID)) * s),
            "reasoning_mask": bf(np.random.uniform(size=(B, S, 1, 1))),
            "Wq": w(), "bq": b(), "Wk": w(), "bk": b(),
            "Wqr": w(), "bqr": b(), "Wkr": w(), "bkr": b()}


def reference(x, reasoning_mask, Wq, bq, Wk, bk, Wqr, bqr, Wkr, bkr):
    xq = mxq(f64(x), 2, "e4m3")
    g = f64(reasoning_mask)

    def proj(W, b):
        return ((xq @ mxq(f64(W), 0, "e4m3")) + f64(b)).reshape(B, S, NH, DH)

    q = proj(Wq, bq)
    k = proj(Wk, bk)
    q_r = proj(Wqr, bqr)
    k_r = proj(Wkr, bkr)
    q = q * (1.0 - g) + q_r * g
    k = k * (1.0 - g) + k_r * g
    return q, k

@@ -1,0 +1,275 @@
+from contextlib import ExitStack
+
+import concourse.mybir as mybir
+from concourse.masks import make_identity
+
+F32 = mybir.dt.float32
+BF16 = mybir.dt.bfloat16
+U32 = mybir.dt.uint32
+U8 = mybir.dt.uint8
+FP8X4 = mybir.dt.float8_e4m3fn_x4
+ALU = mybir.AluOpType
+ACT = mybir.ActivationFunctionType
+
+P = 128
+TOKENS = 4 * 1024
+HID = 1024
+FEAT = 256
+PACK = 4
+K_PASS = P * PACK
+PASSES = HID // K_PASS
+BANK = 2 * FEAT
+WORDS = HID // 2
+TILES = TOKENS // P
+GROUP_TILES = 4
+ROUND_TILES = 2
+ROUNDS = TILES // ROUND_TILES
+PSUM_BANKS = 8
+ACC_PAIRS = (PSUM_BANKS - ROUND_TILES) // 2
+BIAS_LEAD = 3
+
+FLOPS = 2 * TOKENS * HID * 4 * FEAT
+
+
+def tile_reasoningmultiheadattention_pa_t_kernel(
+    tc, x, reasoning_mask, Wq, bq, Wk, bk, Wqr, bqr, Wkr, bkr, out_0, out_1
+):
+    nc = tc.nc
+    weights = (Wq, Wk, Wqr, Wkr)
+    biases = (bq, bk, bqr, bkr)
+
+    x_groups = x.rearrange("b s h -> (b s) h").rearrange(
+        "(a p v) h -> a p (v h)", p=P, v=GROUP_TILES
+    )
+    gate_by_tile = reasoning_mask.rearrange("b s o i -> (b s o i)").rearrange(
+        "(a p v) -> p a v", p=P, v=GROUP_TILES
+    )
+    out_groups = [
+        o.rearrange("b s n d -> (b s) (n d)").rearrange("(a p v) f -> a p v f", p=P, v=GROUP_TILES)
+        for o in (out_0, out_1)
+    ]
+
+    with ExitStack() as ctx:
+        keep = ctx.enter_context(tc.tile_pool(name="keep", bufs=1))
+        x_pool = ctx.enter_context(tc.tile_pool(name="x_pool", bufs=TILES // GROUP_TILES))
+        mx_pool = ctx.enter_context(tc.tile_pool(name="mx_pool", bufs=2))
+        blend_pool = ctx.enter_context(tc.tile_pool(name="blend_pool", bufs=3))
+        xt_pool = ctx.enter_context(tc.psum_pool(name="xt_pool", bufs=ROUND_TILES))
+        acc_pool = ctx.enter_context(tc.psum_pool(name="acc_pool", bufs=ACC_PAIRS))
+        ctx.enter_context(tc.manual_schedule())
+
+        ident = keep.tile([P, P], F32)
+        make_identity(nc, ident[:])
+        ones = keep.tile([P, P], BF16)
+        nc.vector.memset(ones[:], 1.0)
+        bias_rows = keep.tile([P, 2, BANK], BF16)
+        nc.vector.memset(bias_rows[:], 0.0)
+
+        x_sb = {}
+
+        def load_x(a):
+            x_group = x_pool.tile([P, GROUP_TILES * HID], BF16)
+            nc.sync.dma_start(out=x_group[:], in_=x_groups[a])
+            x_sb[a] = x_group
+
+        w_raw = []
+        load_x(0)
+        gate_bf = keep.tile([P, TILES], BF16)
+        nc.sync.dma_start(
+            out=gate_bf[:].rearrange("p (a v) -> p a v", v=GROUP_TILES), in_=gate_by_tile
+        )
+        for bank in range(2):
+            for side in range(2):
+                nc.sync.dma_start(
+                    out=bias_rows[0:1, bank, side * FEAT : (side + 1) * FEAT],
+                    in_=biases[2 * bank + side].unsqueeze(0),
+                )
+        for w in weights:
+            raw = keep.tile([P, PASSES * PACK, FEAT], BF16, name="w_raw%d" % len(w_raw))
+            nc.sync.dma_start(
+                out=raw[:].rearrange("p (j e) n -> p j e n", e=2),
+                in_=w.rearrange("(j p e) n -> p j e n", p=P, e=2),
+            )
+            w_raw.append(raw)
+        for a in range(1, TILES // GROUP_TILES):
+            load_x(a)
+
+        grouped_of = {}
+        codes_of = {}
+        scales_of = {}
+
+        def transpose_round(r):
+            grouped = mx_pool.tile([P, ROUND_TILES * HID], BF16, align_bytes=64)
+            grouped_words = grouped[:].bitcast(F32)
+            for t in range(ROUND_TILES):
+                a, v = divmod(r * ROUND_TILES + t, GROUP_TILES)
+                x_words = x_sb[a][:].bitcast(F32)
+                xt = xt_pool.tile([P, WORDS // P, P], F32)
+                for j in range(WORDS // P):
+                    first = v * WORDS + j * P
+                    nc.tensor.transpose(
+                        out=xt[:, j, :], in_=x_words[:, first : first + P], identity=ident[:]
+                    )
+                nc.scalar.copy(
+                    out=grouped_words[:, t * WORDS : (t + 1) * WORDS].rearrange(
+                        "p (c m u) -> p c m u", c=PASSES, u=2
+                    ),
+                    in_=xt[:].rearrange("p (c u) m -> p c m u", u=2),
+                )
+            grouped_of[r] = grouped
+
+        def quantise_round(r):
+            x_codes = mx_pool.tile([P, ROUND_TILES * PASSES * P], U32, align_bytes=64)
+            x_scales = mx_pool.tile([P, ROUND_TILES * PASSES * P], U8, align_bytes=64)
+            nc.vector.quantize_mx(
+                out=x_codes[:].bitcast(FP8X4), scales=x_scales[:], in_=grouped_of[r][:]
+            )
+            codes_of[r] = x_codes
+            scales_of[r] = x_scales
+
+        blended_bias = {}
+
+        def blend_bias(i):
+            scaled_delta = blend_pool.tile([P, BANK], F32)
+            nc.scalar.activation(
+                out=scaled_delta[:], in_=bias_delta[:], func=ACT.Copy, scale=gate[:, i : i + 1]
+            )
+            bias_tile = blend_pool.tile([P, BANK], F32, bufs=BIAS_LEAD + 2)
+            nc.gpsimd.tensor_tensor(
+                out=bias_tile[:], in0=scaled_delta[:], in1=bias_plain[:], op=ALU.add
+            )
+            blended_bias[i] = bias_tile
+
+        acc_of = {}
+
+        def project_tile(i):
+            r, t = divmod(i, ROUND_TILES)
+            acc_plain = acc_pool.tile([P, BANK], F32)
+            acc_reasoning = acc_pool.tile([P, BANK], F32)
+            for bank, acc in enumerate((acc_plain, acc_reasoning)):
+                for c in range(PASSES):
+                    cols = slice((t * PASSES + c) * P, (t * PASSES + c + 1) * P)
+                    nc.tensor.matmul_mx(
+                        out=acc[:],
+                        lhsT=codes_of[r][:, cols].bitcast(FP8X4),
+                        lhsT_scale=scales_of[r][:, cols],
+                        rhs=w_codes[:, c, bank, :].bitcast(FP8X4),
+                        rhs_scale=w_scales[:, c, bank, :],
+                        start=(c == 0),
+                        stop=(c == PASSES - 1),
+                    )
+            acc_of[i] = (acc_plain, acc_reasoning)
+
+        partial_of = {}
+        result_of = {}
+
+        def blend_plain(i):
+            partial = blend_pool.tile([P, BANK], F32)
+            nc.vector.scalar_tensor_tensor(
+                out=partial[:],
+                in0=acc_of[i][0][:],
+                scalar=one_minus_gate[:, i : i + 1],
+                in1=blended_bias[i][:],
+                op0=ALU.mult,
+                op1=ALU.add,
+            )
+            partial_of[i] = partial
+
+        def blend_reasoning(i):
+            r, t = divmod(i, ROUND_TILES)
+            if t == 0:
+                result = blend_pool.tile([P, 2, ROUND_TILES, FEAT], F32)
+                result_of[r] = result
+            nc.vector.scalar_tensor_tensor(
+                out=result_of[r][:, :, t, :],
+                in0=acc_of[i][1][:].rearrange("p (s f) -> p s f", s=2),
+                scalar=gate[:, i : i + 1],
+                in1=partial_of[i][:].rearrange("p (s f) -> p s f", s=2),
+                op0=ALU.mult,
+                op1=ALU.add,
+            )
+
+        def store_round(r):
+            a, v = divmod(r * ROUND_TILES, GROUP_TILES)
+            for side in range(2):
+                nc.sync.dma_start(
+                    out=out_groups[side][a, :, v : v + ROUND_TILES, :],
+                    in_=result_of[r][:, side, :, :],
+                )
+
+        w_grouped = keep.tile([P, PASSES, 2, BANK, PACK], BF16, align_bytes=64)
+        w_codes = keep.tile([P, PASSES, 2, BANK], U32, align_bytes=64)
+        w_scales = keep.tile([P, PASSES, 2, BANK], U8, align_bytes=64)
+
+        def regroup_weight(bank, side):
+            for c in range(PASSES):
+                rows = w_raw[2 * bank + side][:, c * PACK : (c + 1) * PACK, :].rearrange(
+                    "p t (b i) -> p b t i", i=4
+                )
+                words = w_grouped[:, c, bank, side * FEAT : (side + 1) * FEAT, :].rearrange(
+                    "p (b i) t -> p b t i", i=4
+                )
+                if c == 0:
+                    nc.vector.tensor_copy(out=words, in_=rows)
+                else:
+                    nc.scalar.copy(out=words, in_=rows)
+
+        def quantise_bank(bank):
+            for c in range(PASSES):
+                nc.vector.quantize_mx(
+                    out=w_codes[:, c, bank, :].bitcast(FP8X4),
+                    scales=w_scales[:, c, bank, :],
+                    in_=w_grouped[:, c, bank, :, :].rearrange("p n t -> p (n t)"),
+                )
+
+        transpose_round(0)
+
+        gate = keep.tile([P, TILES], F32)
+        nc.vector.tensor_copy(out=gate[:], in_=gate_bf[:])
+        one_minus_gate = keep.tile([P, TILES], F32)
+        nc.vector.tensor_scalar(
+            out=one_minus_gate[:], in0=gate[:], scalar1=-1.0, scalar2=1.0, op0=ALU.mult, op1=ALU.add
+        )
+
+        regroup_weight(0, 0)
+        quantise_round(0)
+
+        bias_plain = keep.tile([P, BANK], F32)
+        bias_delta = keep.tile([P, BANK], F32)
+        spread_plain = acc_pool.tile([P, BANK], F32, tag="acc_plain")
+        spread_reasoning = acc_pool.tile([P, BANK], F32, tag="acc_reasoning")
+        nc.tensor.matmul(
+            out=spread_plain[:], lhsT=ones[:], rhs=bias_rows[:, 0, :], start=True, stop=True
+        )
+        nc.tensor.matmul(
+            out=spread_reasoning[:], lhsT=ones[:], rhs=bias_rows[:, 1, :], start=True, stop=True
+        )
+        nc.scalar.copy(out=bias_plain[:], in_=spread_plain[:])
+
+        regroup_weight(0, 1)
+        nc.vector.tensor_tensor(
+            out=bias_delta[:], in0=spread_reasoning[:], in1=bias_plain[:], op=ALU.subtract
+        )
+        quantise_bank(0)
+        regroup_weight(1, 0)
+        regroup_weight(1, 1)
+        quantise_bank(1)
+
+        for i in range(BIAS_LEAD):
+            blend_bias(i)
+
+        for r in range(ROUNDS):
+            if r + 1 < ROUNDS:
+                transpose_round(r + 1)
+            for t in range(ROUND_TILES):
+                i = r * ROUND_TILES + t
+                if i + BIAS_LEAD < TILES:
+                    blend_bias(i + BIAS_LEAD)
+                project_tile(i)
+                blend_plain(i)
+                if t > 0:
+                    blend_reasoning(i - 1)
+                elif r + 1 < ROUNDS:
+                    quantise_round(r + 1)
+            blend_reasoning(r * ROUND_TILES + ROUND_TILES - 1)
+            store_round(r)

@@ -26,7 +26,7 @@ ROUND_TILES = 2
 ROUNDS = TILES // ROUND_TILES
 PSUM_BANKS = 8
 ACC_PAIRS = (PSUM_BANKS - ROUND_TILES) // 2
-BIAS_LEAD = 3
+BIAS_LEAD = 2
 
 FLOPS = 2 * TOKENS * HID * 4 * FEAT
 
@@ -129,16 +129,24 @@ def tile_reasoningmultiheadattention_pa_t_kernel(
 
         blended_bias = {}
 
-        def blend_bias(i):
-            scaled_delta = blend_pool.tile([P, BANK], F32)
-            nc.scalar.activation(
-                out=scaled_delta[:], in_=bias_delta[:], func=ACT.Copy, scale=gate[:, i : i + 1]
-            )
-            bias_tile = blend_pool.tile([P, BANK], F32, bufs=BIAS_LEAD + 2)
+        def blend_bias(r):
+            scaled_delta = blend_pool.tile([P, ROUND_TILES, BANK], F32)
+            for t in range(ROUND_TILES):
+                i = r * ROUND_TILES + t
+                nc.scalar.activation(
+                    out=scaled_delta[:, t, :],
+                    in_=bias_delta[:],
+                    func=ACT.Copy,
+                    scale=gate[:, i : i + 1],
+                )
+            bias_round = blend_pool.tile([P, ROUND_TILES, BANK], F32, bufs=BIAS_LEAD + 2)
             nc.gpsimd.tensor_tensor(
-                out=bias_tile[:], in0=scaled_delta[:], in1=bias_plain[:], op=ALU.add
+                out=bias_round[:],
+                in0=scaled_delta[:],
+                in1=bias_plain[:].unsqueeze(1).to_broadcast([P, ROUND_TILES, BANK]),
+                op=ALU.add,
             )
-            blended_bias[i] = bias_tile
+            blended_bias[r] = bias_round
 
         acc_of = {}
 
@@ -169,7 +177,7 @@ def tile_reasoningmultiheadattention_pa_t_kernel(
                 out=partial[:],
                 in0=acc_of[i][0][:],
                 scalar=one_minus_gate[:, i : i + 1],
-                in1=blended_bias[i][:],
+                in1=blended_bias[i // ROUND_TILES][:, i % ROUND_TILES, :],
                 op0=ALU.mult,
                 op1=ALU.add,
             )
@@ -255,16 +263,16 @@ def tile_reasoningmultiheadattention_pa_t_kernel(
         regroup_weight(1, 1)
         quantise_bank(1)
 
-        for i in range(BIAS_LEAD):
-            blend_bias(i)
+        for r in range(BIAS_LEAD):
+            blend_bias(r)
 
         for r in range(ROUNDS):
             if r + 1 < ROUNDS:
                 transpose_round(r + 1)
+            if r + BIAS_LEAD < ROUNDS:
+                blend_bias(r + BIAS_LEAD)
             for t in range(ROUND_TILES):
                 i = r * ROUND_TILES + t
-                if i + BIAS_LEAD < TILES:
-                    blend_bias(i + BIAS_LEAD)
                 project_tile(i)
                 blend_plain(i)
                 if t > 0:

@@ -21,12 +21,12 @@ PASSES = HID // K_PASS
 BANK = 2 * FEAT
 WORDS = HID // 2
 TILES = TOKENS // P
-GROUP_TILES = 4
 ROUND_TILES = 2
 ROUNDS = TILES // ROUND_TILES
 PSUM_BANKS = 8
-ACC_PAIRS = (PSUM_BANKS - ROUND_TILES) // 2
+ACC_BUFS = (PSUM_BANKS - ROUND_TILES) // 2
 BIAS_LEAD = 2
+PLAIN, REASONING = 0, 1
 
 FLOPS = 2 * TOKENS * HID * 4 * FEAT
 
@@ -38,52 +38,49 @@ def tile_reasoningmultiheadattention_pa_t_kernel(
     weights = (Wq, Wk, Wqr, Wkr)
     biases = (bq, bk, bqr, bkr)
 
-    x_groups = x.rearrange("b s h -> (b s) h").rearrange(
-        "(a p v) h -> a p (v h)", p=P, v=GROUP_TILES
-    )
-    gate_by_tile = reasoning_mask.rearrange("b s o i -> (b s o i)").rearrange(
-        "(a p v) -> p a v", p=P, v=GROUP_TILES
-    )
-    out_groups = [
-        o.rearrange("b s n d -> (b s) (n d)").rearrange("(a p v) f -> a p v f", p=P, v=GROUP_TILES)
+    x_tiles = x.rearrange("b s h -> (b s) h").rearrange("(p i) h -> p i h", p=P)
+    gate_tiles = reasoning_mask.rearrange("b s o i -> (b s o i)").rearrange("(p i) -> p i", p=P)
+    out_tiles = [
+        o.rearrange("b s n d -> (b s) (n d)").rearrange("(p i) f -> p i f", p=P)
         for o in (out_0, out_1)
     ]
 
     with ExitStack() as ctx:
         keep = ctx.enter_context(tc.tile_pool(name="keep", bufs=1))
-        x_pool = ctx.enter_context(tc.tile_pool(name="x_pool", bufs=TILES // GROUP_TILES))
-        mx_pool = ctx.enter_context(tc.tile_pool(name="mx_pool", bufs=2))
+        x_pool = ctx.enter_context(tc.tile_pool(name="x_pool", bufs=ROUNDS))
+        mx_pool = ctx.enter_context(tc.tile_pool(name="mx_pool", bufs=3))
         blend_pool = ctx.enter_context(tc.tile_pool(name="blend_pool", bufs=3))
         xt_pool = ctx.enter_context(tc.psum_pool(name="xt_pool", bufs=ROUND_TILES))
-        acc_pool = ctx.enter_context(tc.psum_pool(name="acc_pool", bufs=ACC_PAIRS))
+        acc_pool = ctx.enter_context(tc.psum_pool(name="acc_pool", bufs=ACC_BUFS))
         ctx.enter_context(tc.manual_schedule())
 
-        ident = keep.tile([P, P], F32)
-        make_identity(nc, ident[:])
-        ones = keep.tile([P, P], BF16)
-        nc.vector.memset(ones[:], 1.0)
         bias_rows = keep.tile([P, 2, BANK], BF16)
         nc.vector.memset(bias_rows[:], 0.0)
+        ones = keep.tile([P, P], BF16)
+        nc.vector.memset(ones[:], 1.0)
+        ident = keep.tile([P, P], F32)
+        make_identity(nc, ident[:])
 
-        x_sb = {}
-
-        def load_x(a):
-            x_group = x_pool.tile([P, GROUP_TILES * HID], BF16)
-            nc.sync.dma_start(out=x_group[:], in_=x_groups[a])
-            x_sb[a] = x_group
-
-        w_raw = []
-        load_x(0)
         gate_bf = keep.tile([P, TILES], BF16)
-        nc.sync.dma_start(
-            out=gate_bf[:].rearrange("p (a v) -> p a v", v=GROUP_TILES), in_=gate_by_tile
-        )
-        for bank in range(2):
+        nc.scalar.dma_start(out=gate_bf[:], in_=gate_tiles)
+        for bank in (PLAIN, REASONING):
             for side in range(2):
-                nc.sync.dma_start(
+                nc.scalar.dma_start(
                     out=bias_rows[0:1, bank, side * FEAT : (side + 1) * FEAT],
                     in_=biases[2 * bank + side].unsqueeze(0),
                 )
+
+        x_sb = {}
+
+        def load_x(r):
+            x_round = x_pool.tile([P, ROUND_TILES, HID], BF16)
+            nc.sync.dma_start(
+                out=x_round[:], in_=x_tiles[:, r * ROUND_TILES : (r + 1) * ROUND_TILES, :]
+            )
+            x_sb[r] = x_round
+
+        w_raw = []
+        load_x(0)
         for w in weights:
             raw = keep.tile([P, PASSES * PACK, FEAT], BF16, name="w_raw%d" % len(w_raw))
             nc.sync.dma_start(
@@ -91,8 +88,8 @@ def tile_reasoningmultiheadattention_pa_t_kernel(
                 in_=w.rearrange("(j p e) n -> p j e n", p=P, e=2),
             )
             w_raw.append(raw)
-        for a in range(1, TILES // GROUP_TILES):
-            load_x(a)
+        for r in range(1, ROUNDS):
+            load_x(r)
 
         grouped_of = {}
         codes_of = {}
@@ -101,12 +98,11 @@ def tile_reasoningmultiheadattention_pa_t_kernel(
         def transpose_round(r):
             grouped = mx_pool.tile([P, ROUND_TILES * HID], BF16, align_bytes=64)
             grouped_words = grouped[:].bitcast(F32)
+            x_words = x_sb[r][:].rearrange("p t h -> p (t h)").bitcast(F32)
             for t in range(ROUND_TILES):
-                a, v = divmod(r * ROUND_TILES + t, GROUP_TILES)
-                x_words = x_sb[a][:].bitcast(F32)
                 xt = xt_pool.tile([P, WORDS // P, P], F32)
                 for j in range(WORDS // P):
-                    first = v * WORDS + j * P
+                    first = t * WORDS + j * P
                     nc.tensor.transpose(
                         out=xt[:, j, :], in_=x_words[:, first : first + P], identity=ident[:]
                     )
@@ -126,84 +122,6 @@ def tile_reasoningmultiheadattention_pa_t_kernel(
             )
             codes_of[r] = x_codes
             scales_of[r] = x_scales
-
-        blended_bias = {}
-
-        def blend_bias(r):
-            scaled_delta = blend_pool.tile([P, ROUND_TILES, BANK], F32)
-            for t in range(ROUND_TILES):
-                i = r * ROUND_TILES + t
-                nc.scalar.activation(
-                    out=scaled_delta[:, t, :],
-                    in_=bias_delta[:],
-                    func=ACT.Copy,
-                    scale=gate[:, i : i + 1],
-                )
-            bias_round = blend_pool.tile([P, ROUND_TILES, BANK], F32, bufs=BIAS_LEAD + 2)
-            nc.gpsimd.tensor_tensor(
-                out=bias_round[:],
-                in0=scaled_delta[:],
-                in1=bias_plain[:].unsqueeze(1).to_broadcast([P, ROUND_TILES, BANK]),
-                op=ALU.add,
-            )
-            blended_bias[r] = bias_round
-
-        acc_of = {}
-
-        def project_tile(i):
-            r, t = divmod(i, ROUND_TILES)
-            acc_plain = acc_pool.tile([P, BANK], F32)
-            acc_reasoning = acc_pool.tile([P, BANK], F32)
-            for bank, acc in enumerate((acc_plain, acc_reasoning)):
-                for c in range(PASSES):
-                    cols = slice((t * PASSES + c) * P, (t * PASSES + c + 1) * P)
-                    nc.tensor.matmul_mx(
-                        out=acc[:],
-                        lhsT=codes_of[r][:, cols].bitcast(FP8X4),
-                        lhsT_scale=scales_of[r][:, cols],
-                        rhs=w_codes[:, c, bank, :].bitcast(FP8X4),
-                        rhs_scale=w_scales[:, c, bank, :],
-                        start=(c == 0),
-                        stop=(c == PASSES - 1),
-                    )
-            acc_of[i] = (acc_plain, acc_reasoning)
-
-        partial_of = {}
-        result_of = {}
-
-        def blend_plain(i):
-            partial = blend_pool.tile([P, BANK], F32)
-            nc.vector.scalar_tensor_tensor(
-                out=partial[:],
-                in0=acc_of[i][0][:],
-                scalar=one_minus_gate[:, i : i + 1],
-                in1=blended_bias[i // ROUND_TILES][:, i % ROUND_TILES, :],
-                op0=ALU.mult,
-                op1=ALU.add,
-            )
-            partial_of[i] = partial
-
-        def blend_reasoning(i):
-            r, t = divmod(i, ROUND_TILES)
-            if t == 0:
-                result = blend_pool.tile([P, 2, ROUND_TILES, FEAT], F32)
-                result_of[r] = result
-            nc.vector.scalar_tensor_tensor(
-                out=result_of[r][:, :, t, :],
-                in0=acc_of[i][1][:].rearrange("p (s f) -> p s f", s=2),
-                scalar=gate[:, i : i + 1],
-                in1=partial_of[i][:].rearrange("p (s f) -> p s f", s=2),
-                op0=ALU.mult,
-                op1=ALU.add,
-            )
-
-        def store_round(r):
-            a, v = divmod(r * ROUND_TILES, GROUP_TILES)
-            for side in range(2):
-                nc.sync.dma_start(
-                    out=out_groups[side][a, :, v : v + ROUND_TILES, :],
-                    in_=result_of[r][:, side, :, :],
-                )
 
         w_grouped = keep.tile([P, PASSES, 2, BANK, PACK], BF16, align_bytes=64)
         w_codes = keep.tile([P, PASSES, 2, BANK], U32, align_bytes=64)
@@ -230,54 +148,142 @@ def tile_reasoningmultiheadattention_pa_t_kernel(
                     in_=w_grouped[:, c, bank, :, :].rearrange("p n t -> p (n t)"),
                 )
 
+        bias_plain = keep.tile([P, BANK], F32)
+        bias_delta = keep.tile([P, BANK], F32)
+        gate = keep.tile([P, TILES], F32)
+        one_minus_gate = keep.tile([P, TILES], F32)
+        blended_bias = {}
+
+        def blend_bias(r):
+            scaled_delta = blend_pool.tile([P, ROUND_TILES, BANK], F32)
+            for t in range(ROUND_TILES):
+                i = r * ROUND_TILES + t
+                nc.scalar.activation(
+                    out=scaled_delta[:, t, :],
+                    in_=bias_delta[:],
+                    func=ACT.Copy,
+                    scale=gate[:, i : i + 1],
+                )
+            bias_round = blend_pool.tile([P, ROUND_TILES, BANK], F32, bufs=BIAS_LEAD + 2)
+            nc.gpsimd.tensor_tensor(
+                out=bias_round[:],
+                in0=scaled_delta[:],
+                in1=bias_plain[:].unsqueeze(1).to_broadcast([P, ROUND_TILES, BANK]),
+                op=ALU.add,
+            )
+            blended_bias[r] = bias_round
+
+        acc_of = {}
+
+        def project_round(r, bank):
+            for t in range(ROUND_TILES):
+                acc = acc_pool.tile([P, BANK], F32, tag="acc%d" % bank)
+                for c in range(PASSES):
+                    cols = slice((t * PASSES + c) * P, (t * PASSES + c + 1) * P)
+                    nc.tensor.matmul_mx(
+                        out=acc[:],
+                        lhsT=codes_of[r][:, cols].bitcast(FP8X4),
+                        lhsT_scale=scales_of[r][:, cols],
+                        rhs=w_codes[:, c, bank, :].bitcast(FP8X4),
+                        rhs_scale=w_scales[:, c, bank, :],
+                        start=(c == 0),
+                        stop=(c == PASSES - 1),
+                    )
+                acc_of[(r, t, bank)] = acc
+
+        partial_of = {}
+        result_of = {}
+
+        def blend_plain(r, t):
+            i = r * ROUND_TILES + t
+            partial = blend_pool.tile([P, BANK], F32, bufs=2 * ROUND_TILES + 1)
+            nc.vector.scalar_tensor_tensor(
+                out=partial[:],
+                in0=acc_of[(r, t, PLAIN)][:],
+                scalar=one_minus_gate[:, i : i + 1],
+                in1=blended_bias[r][:, t, :],
+                op0=ALU.mult,
+                op1=ALU.add,
+            )
+            partial_of[(r, t)] = partial
+
+        def blend_reasoning(r, t):
+            i = r * ROUND_TILES + t
+            if t == 0:
+                result = blend_pool.tile([P, 2, ROUND_TILES, FEAT], F32)
+                result_of[r] = result
+            nc.vector.scalar_tensor_tensor(
+                out=result_of[r][:, :, t, :],
+                in0=acc_of[(r, t, REASONING)][:].rearrange("p (s f) -> p s f", s=2),
+                scalar=gate[:, i : i + 1],
+                in1=partial_of[(r, t)][:].rearrange("p (s f) -> p s f", s=2),
+                op0=ALU.mult,
+                op1=ALU.add,
+            )
+
+        def finish_round(r):
+            project_round(r, REASONING)
+            for t in range(ROUND_TILES):
+                blend_reasoning(r, t)
+            for side in range(2):
+                nc.sync.dma_start(
+                    out=out_tiles[side][:, r * ROUND_TILES : (r + 1) * ROUND_TILES, :],
+                    in_=result_of[r][:, side, :, :],
+                )
+
         transpose_round(0)
 
-        gate = keep.tile([P, TILES], F32)
+        spread_plain = acc_pool.tile([P, BANK], F32, tag="acc0")
+        spread_reasoning = acc_pool.tile([P, BANK], F32, tag="acc1")
+        nc.tensor.matmul(
+            out=spread_plain[:], lhsT=ones[:], rhs=bias_rows[:, PLAIN, :], start=True, stop=True
+        )
+        nc.tensor.matmul(
+            out=spread_reasoning[:],
+            lhsT=ones[:],
+            rhs=bias_rows[:, REASONING, :],
+            start=True,
+            stop=True,
+        )
+        nc.scalar.copy(out=bias_plain[:], in_=spread_plain[:])
         nc.vector.tensor_copy(out=gate[:], in_=gate_bf[:])
-        one_minus_gate = keep.tile([P, TILES], F32)
         nc.vector.tensor_scalar(
             out=one_minus_gate[:], in0=gate[:], scalar1=-1.0, scalar2=1.0, op0=ALU.mult, op1=ALU.add
         )
-
-        regroup_weight(0, 0)
-        quantise_round(0)
-
-        bias_plain = keep.tile([P, BANK], F32)
-        bias_delta = keep.tile([P, BANK], F32)
-        spread_plain = acc_pool.tile([P, BANK], F32, tag="acc_plain")
-        spread_reasoning = acc_pool.tile([P, BANK], F32, tag="acc_reasoning")
-        nc.tensor.matmul(
-            out=spread_plain[:], lhsT=ones[:], rhs=bias_rows[:, 0, :], start=True, stop=True
-        )
-        nc.tensor.matmul(
-            out=spread_reasoning[:], lhsT=ones[:], rhs=bias_rows[:, 1, :], start=True, stop=True
-        )
-        nc.scalar.copy(out=bias_plain[:], in_=spread_plain[:])
-
-        regroup_weight(0, 1)
         nc.vector.tensor_tensor(
             out=bias_delta[:], in0=spread_reasoning[:], in1=bias_plain[:], op=ALU.subtract
         )
-        quantise_bank(0)
-        regroup_weight(1, 0)
-        regroup_weight(1, 1)
-        quantise_bank(1)
 
-        for r in range(BIAS_LEAD):
-            blend_bias(r)
+        regroup_weight(PLAIN, 0)
+        quantise_round(0)
+        regroup_weight(PLAIN, 1)
+        blend_bias(0)
+        quantise_bank(PLAIN)
 
-        for r in range(ROUNDS):
+        def start_round(r):
             if r + 1 < ROUNDS:
                 transpose_round(r + 1)
+            project_round(r, PLAIN)
+
+        def blend_plain_round(r):
+            blend_plain(r, 0)
+            if r + 1 < ROUNDS:
+                quantise_round(r + 1)
+            for t in range(1, ROUND_TILES):
+                blend_plain(r, t)
+
+        start_round(0)
+        regroup_weight(REASONING, 0)
+        regroup_weight(REASONING, 1)
+        for r in range(1, BIAS_LEAD + 1):
+            blend_bias(r)
+        blend_plain_round(0)
+        quantise_bank(REASONING)
+
+        for r in range(1, ROUNDS):
+            start_round(r)
             if r + BIAS_LEAD < ROUNDS:
                 blend_bias(r + BIAS_LEAD)
-            for t in range(ROUND_TILES):
-                i = r * ROUND_TILES + t
-                project_tile(i)
-                blend_plain(i)
-                if t > 0:
-                    blend_reasoning(i - 1)
-                elif r + 1 < ROUNDS:
-                    quantise_round(r + 1)
-            blend_reasoning(r * ROUND_TILES + ROUND_TILES - 1)
-            store_round(r)
+            blend_plain_round(r)
+            finish_round(r - 1)
+        finish_round(ROUNDS - 1)

@@ -21,11 +21,14 @@ PASSES = HID // K_PASS
 BANK = 2 * FEAT
 WORDS = HID // 2
 TILES = TOKENS // P
+GROUP_TILES = 4
 ROUND_TILES = 2
 ROUNDS = TILES // ROUND_TILES
+LAST = ROUNDS - 1
+TOKEN_LEAD = 2
 PSUM_BANKS = 8
-ACC_BUFS = (PSUM_BANKS - ROUND_TILES) // 2
-BIAS_LEAD = 2
+ACC_BANKS = PSUM_BANKS - ROUND_TILES
+RESULT_BUFS = 6
 PLAIN, REASONING = 0, 1
 
 FLOPS = 2 * TOKENS * HID * 4 * FEAT
@@ -38,20 +41,24 @@ def tile_reasoningmultiheadattention_pa_t_kernel(
     weights = (Wq, Wk, Wqr, Wkr)
     biases = (bq, bk, bqr, bkr)
 
-    x_tiles = x.rearrange("b s h -> (b s) h").rearrange("(p i) h -> p i h", p=P)
-    gate_tiles = reasoning_mask.rearrange("b s o i -> (b s o i)").rearrange("(p i) -> p i", p=P)
-    out_tiles = [
-        o.rearrange("b s n d -> (b s) (n d)").rearrange("(p i) f -> p i f", p=P)
+    x_groups = x.rearrange("b s h -> (b s) h").rearrange(
+        "(a p v) h -> a p v h", p=P, v=GROUP_TILES
+    )
+    gate_tiles = reasoning_mask.rearrange("b s o i -> (b s o i)").rearrange(
+        "(a p v) -> p a v", p=P, v=GROUP_TILES
+    )
+    out_groups = [
+        o.rearrange("b s n d -> (b s) (n d)").rearrange("(a p v) f -> a p v f", p=P, v=GROUP_TILES)
         for o in (out_0, out_1)
     ]
 
     with ExitStack() as ctx:
         keep = ctx.enter_context(tc.tile_pool(name="keep", bufs=1))
         x_pool = ctx.enter_context(tc.tile_pool(name="x_pool", bufs=ROUNDS))
-        mx_pool = ctx.enter_context(tc.tile_pool(name="mx_pool", bufs=3))
+        mx_pool = ctx.enter_context(tc.tile_pool(name="mx_pool", bufs=TOKEN_LEAD + 2))
         blend_pool = ctx.enter_context(tc.tile_pool(name="blend_pool", bufs=3))
         xt_pool = ctx.enter_context(tc.psum_pool(name="xt_pool", bufs=ROUND_TILES))
-        acc_pool = ctx.enter_context(tc.psum_pool(name="acc_pool", bufs=ACC_BUFS))
+        acc_pool = ctx.enter_context(tc.psum_pool(name="acc_pool", bufs=ACC_BANKS))
         ctx.enter_context(tc.manual_schedule())
 
         bias_rows = keep.tile([P, 2, BANK], BF16)
@@ -61,41 +68,47 @@ def tile_reasoningmultiheadattention_pa_t_kernel(
         ident = keep.tile([P, P], F32)
         make_identity(nc, ident[:])
 
-        gate_bf = keep.tile([P, TILES], BF16)
-        nc.scalar.dma_start(out=gate_bf[:], in_=gate_tiles)
+        x_sb = {}
+
+        def load_tokens(r):
+            a, v = divmod(r * ROUND_TILES, GROUP_TILES)
+            x_round = x_pool.tile([P, ROUND_TILES, HID], BF16)
+            nc.sync.dma_start(out=x_round[:], in_=x_groups[a, :, v : v + ROUND_TILES, :])
+            x_sb[r] = x_round
+
+        w_raw = {}
+
+        def load_weights(bank):
+            for side in range(2):
+                raw = keep.tile([P, PASSES * PACK, FEAT], BF16, name="w_raw%d%d" % (bank, side))
+                nc.sync.dma_start(
+                    out=raw[:].rearrange("p (j e) n -> p j e n", e=2),
+                    in_=weights[2 * bank + side].rearrange("(j p e) n -> p j e n", p=P, e=2),
+                )
+                w_raw[(bank, side)] = raw
+
+        load_tokens(0)
+        load_weights(PLAIN)
         for bank in (PLAIN, REASONING):
             for side in range(2):
                 nc.scalar.dma_start(
                     out=bias_rows[0:1, bank, side * FEAT : (side + 1) * FEAT],
                     in_=biases[2 * bank + side].unsqueeze(0),
                 )
-
-        x_sb = {}
-
-        def load_x(r):
-            x_round = x_pool.tile([P, ROUND_TILES, HID], BF16)
-            nc.sync.dma_start(
-                out=x_round[:], in_=x_tiles[:, r * ROUND_TILES : (r + 1) * ROUND_TILES, :]
-            )
-            x_sb[r] = x_round
-
-        w_raw = []
-        load_x(0)
-        for w in weights:
-            raw = keep.tile([P, PASSES * PACK, FEAT], BF16, name="w_raw%d" % len(w_raw))
-            nc.sync.dma_start(
-                out=raw[:].rearrange("p (j e) n -> p j e n", e=2),
-                in_=w.rearrange("(j p e) n -> p j e n", p=P, e=2),
-            )
-            w_raw.append(raw)
-        for r in range(1, ROUNDS):
-            load_x(r)
+        gate_bf = keep.tile([P, TILES], BF16)
+        nc.scalar.dma_start(
+            out=gate_bf[:].rearrange("p (a v) -> p a v", v=GROUP_TILES), in_=gate_tiles
+        )
+        load_tokens(1)
+        load_weights(REASONING)
+        for r in range(2, ROUNDS):
+            load_tokens(r)
 
         grouped_of = {}
         codes_of = {}
         scales_of = {}
 
-        def transpose_round(r):
+        def transpose_tokens(r):
             grouped = mx_pool.tile([P, ROUND_TILES * HID], BF16, align_bytes=64)
             grouped_words = grouped[:].bitcast(F32)
             x_words = x_sb[r][:].rearrange("p t h -> p (t h)").bitcast(F32)
@@ -114,7 +127,7 @@ def tile_reasoningmultiheadattention_pa_t_kernel(
                 )
             grouped_of[r] = grouped
 
-        def quantise_round(r):
+        def quantise_tokens(r):
             x_codes = mx_pool.tile([P, ROUND_TILES * PASSES * P], U32, align_bytes=64)
             x_scales = mx_pool.tile([P, ROUND_TILES * PASSES * P], U8, align_bytes=64)
             nc.vector.quantize_mx(
@@ -127,20 +140,21 @@ def tile_reasoningmultiheadattention_pa_t_kernel(
         w_codes = keep.tile([P, PASSES, 2, BANK], U32, align_bytes=64)
         w_scales = keep.tile([P, PASSES, 2, BANK], U8, align_bytes=64)
 
-        def regroup_weight(bank, side):
-            for c in range(PASSES):
-                rows = w_raw[2 * bank + side][:, c * PACK : (c + 1) * PACK, :].rearrange(
-                    "p t (b i) -> p b t i", i=4
-                )
-                words = w_grouped[:, c, bank, side * FEAT : (side + 1) * FEAT, :].rearrange(
-                    "p (b i) t -> p b t i", i=4
-                )
-                if c == 0:
-                    nc.vector.tensor_copy(out=words, in_=rows)
-                else:
-                    nc.scalar.copy(out=words, in_=rows)
+        def regroup_weights(bank):
+            for side in range(2):
+                for c in range(PASSES):
+                    rows = w_raw[(bank, side)][:, c * PACK : (c + 1) * PACK, :].rearrange(
+                        "p t (b i) -> p b t i", i=4
+                    )
+                    words = w_grouped[:, c, bank, side * FEAT : (side + 1) * FEAT, :].rearrange(
+                        "p (b i) t -> p b t i", i=4
+                    )
+                    if bank == REASONING and c == 1:
+                        nc.scalar.copy(out=words, in_=rows)
+                    else:
+                        nc.vector.tensor_copy(out=words, in_=rows)
 
-        def quantise_bank(bank):
+        def quantise_weights(bank):
             for c in range(PASSES):
                 nc.vector.quantize_mx(
                     out=w_codes[:, c, bank, :].bitcast(FP8X4),
@@ -148,93 +162,84 @@ def tile_reasoningmultiheadattention_pa_t_kernel(
                     in_=w_grouped[:, c, bank, :, :].rearrange("p n t -> p (n t)"),
                 )
 
-        bias_plain = keep.tile([P, BANK], F32)
-        bias_delta = keep.tile([P, BANK], F32)
+        def project(r, t, bank):
+            acc = acc_pool.tile([P, BANK], F32)
+            for c in range(PASSES):
+                cols = slice((t * PASSES + c) * P, (t * PASSES + c + 1) * P)
+                nc.tensor.matmul_mx(
+                    out=acc[:],
+                    lhsT=codes_of[r][:, cols].bitcast(FP8X4),
+                    lhsT_scale=scales_of[r][:, cols],
+                    rhs=w_codes[:, c, bank, :].bitcast(FP8X4),
+                    rhs_scale=w_scales[:, c, bank, :],
+                    start=(c == 0),
+                    stop=(c == PASSES - 1),
+                )
+            return acc[:].rearrange("p (s f) -> p s f", s=2)
+
+        bias_plain = keep.tile([P, 2, FEAT], F32)
+        bias_delta = keep.tile([P, 2, FEAT], F32)
         gate = keep.tile([P, TILES], F32)
         one_minus_gate = keep.tile([P, TILES], F32)
-        blended_bias = {}
 
-        def blend_bias(r):
-            scaled_delta = blend_pool.tile([P, ROUND_TILES, BANK], F32)
+        def plain_half(r, bias_of_tile):
+            partials = []
+            for t in range(ROUND_TILES):
+                i = r * ROUND_TILES + t
+                partial = blend_pool.tile([P, 2, FEAT], F32)
+                nc.vector.scalar_tensor_tensor(
+                    out=partial[:],
+                    in0=project(r, t, PLAIN),
+                    scalar=one_minus_gate[:, i : i + 1],
+                    in1=bias_of_tile[t],
+                    op0=ALU.mult,
+                    op1=ALU.add,
+                )
+                partials.append(partial)
+            return partials
+
+        round_shape = [P, 2, ROUND_TILES, FEAT]
+
+        def reasoning_half(r, partials):
+            blended = blend_pool.tile(round_shape, F32)
+            for t in range(ROUND_TILES):
+                i = r * ROUND_TILES + t
+                nc.vector.scalar_tensor_tensor(
+                    out=blended[:, :, t, :],
+                    in0=project(r, t, REASONING),
+                    scalar=gate[:, i : i + 1],
+                    in1=partials[t][:],
+                    op0=ALU.mult,
+                    op1=ALU.add,
+                )
+            return blended
+
+        def scale_delta(r):
+            scaled_delta = blend_pool.tile(round_shape, F32)
             for t in range(ROUND_TILES):
                 i = r * ROUND_TILES + t
                 nc.scalar.activation(
-                    out=scaled_delta[:, t, :],
+                    out=scaled_delta[:, :, t, :],
                     in_=bias_delta[:],
                     func=ACT.Copy,
                     scale=gate[:, i : i + 1],
                 )
-            bias_round = blend_pool.tile([P, ROUND_TILES, BANK], F32, bufs=BIAS_LEAD + 2)
-            nc.gpsimd.tensor_tensor(
-                out=bias_round[:],
-                in0=scaled_delta[:],
-                in1=bias_plain[:].unsqueeze(1).to_broadcast([P, ROUND_TILES, BANK]),
-                op=ALU.add,
-            )
-            blended_bias[r] = bias_round
+            return scaled_delta
 
-        acc_of = {}
-
-        def project_round(r, bank):
-            for t in range(ROUND_TILES):
-                acc = acc_pool.tile([P, BANK], F32, tag="acc%d" % bank)
-                for c in range(PASSES):
-                    cols = slice((t * PASSES + c) * P, (t * PASSES + c + 1) * P)
-                    nc.tensor.matmul_mx(
-                        out=acc[:],
-                        lhsT=codes_of[r][:, cols].bitcast(FP8X4),
-                        lhsT_scale=scales_of[r][:, cols],
-                        rhs=w_codes[:, c, bank, :].bitcast(FP8X4),
-                        rhs_scale=w_scales[:, c, bank, :],
-                        start=(c == 0),
-                        stop=(c == PASSES - 1),
-                    )
-                acc_of[(r, t, bank)] = acc
-
-        partial_of = {}
-        result_of = {}
-
-        def blend_plain(r, t):
-            i = r * ROUND_TILES + t
-            partial = blend_pool.tile([P, BANK], F32, bufs=2 * ROUND_TILES + 1)
-            nc.vector.scalar_tensor_tensor(
-                out=partial[:],
-                in0=acc_of[(r, t, PLAIN)][:],
-                scalar=one_minus_gate[:, i : i + 1],
-                in1=blended_bias[r][:, t, :],
-                op0=ALU.mult,
-                op1=ALU.add,
-            )
-            partial_of[(r, t)] = partial
-
-        def blend_reasoning(r, t):
-            i = r * ROUND_TILES + t
-            if t == 0:
-                result = blend_pool.tile([P, 2, ROUND_TILES, FEAT], F32)
-                result_of[r] = result
-            nc.vector.scalar_tensor_tensor(
-                out=result_of[r][:, :, t, :],
-                in0=acc_of[(r, t, REASONING)][:].rearrange("p (s f) -> p s f", s=2),
-                scalar=gate[:, i : i + 1],
-                in1=partial_of[(r, t)][:].rearrange("p (s f) -> p s f", s=2),
-                op0=ALU.mult,
-                op1=ALU.add,
-            )
-
-        def finish_round(r):
-            project_round(r, REASONING)
-            for t in range(ROUND_TILES):
-                blend_reasoning(r, t)
+        def store(r, result):
+            a, v = divmod(r * ROUND_TILES, GROUP_TILES)
             for side in range(2):
                 nc.sync.dma_start(
-                    out=out_tiles[side][:, r * ROUND_TILES : (r + 1) * ROUND_TILES, :],
-                    in_=result_of[r][:, side, :, :],
+                    out=out_groups[side][a, :, v : v + ROUND_TILES, :], in_=result[:, side, :, :]
                 )
 
-        transpose_round(0)
+        transpose_tokens(0)
+        regroup_weights(PLAIN)
+        quantise_tokens(0)
+        quantise_weights(PLAIN)
 
-        spread_plain = acc_pool.tile([P, BANK], F32, tag="acc0")
-        spread_reasoning = acc_pool.tile([P, BANK], F32, tag="acc1")
+        spread_plain = acc_pool.tile([P, BANK], F32, tag="acc")
+        spread_reasoning = acc_pool.tile([P, BANK], F32, tag="acc")
         nc.tensor.matmul(
             out=spread_plain[:], lhsT=ones[:], rhs=bias_rows[:, PLAIN, :], start=True, stop=True
         )
@@ -245,45 +250,41 @@ def tile_reasoningmultiheadattention_pa_t_kernel(
             start=True,
             stop=True,
         )
-        nc.scalar.copy(out=bias_plain[:], in_=spread_plain[:])
-        nc.vector.tensor_copy(out=gate[:], in_=gate_bf[:])
-        nc.vector.tensor_scalar(
-            out=one_minus_gate[:], in0=gate[:], scalar1=-1.0, scalar2=1.0, op0=ALU.mult, op1=ALU.add
+        nc.scalar.copy(out=bias_plain[:].rearrange("p s f -> p (s f)"), in_=spread_plain[:])
+        nc.scalar.copy(out=gate[:], in_=gate_bf[:])
+        nc.scalar.activation(
+            out=one_minus_gate[:], in_=gate_bf[:], func=ACT.Copy, bias=1.0, scale=-1.0
         )
         nc.vector.tensor_tensor(
-            out=bias_delta[:], in0=spread_reasoning[:], in1=bias_plain[:], op=ALU.subtract
+            out=bias_delta[:].rearrange("p s f -> p (s f)"),
+            in0=spread_reasoning[:],
+            in1=bias_plain[:].rearrange("p s f -> p (s f)"),
+            op=ALU.subtract,
         )
 
-        regroup_weight(PLAIN, 0)
-        quantise_round(0)
-        regroup_weight(PLAIN, 1)
-        blend_bias(0)
-        quantise_bank(PLAIN)
+        transpose_tokens(1)
+        regroup_weights(REASONING)
+        quantise_tokens(1)
+        quantise_weights(REASONING)
 
-        def start_round(r):
-            if r + 1 < ROUNDS:
-                transpose_round(r + 1)
-            project_round(r, PLAIN)
+        last_bias = keep.tile(round_shape, F32)
+        nc.gpsimd.tensor_tensor(
+            out=last_bias[:],
+            in0=scale_delta(LAST)[:],
+            in1=bias_plain[:].unsqueeze(2).to_broadcast(round_shape),
+            op=ALU.add,
+        )
 
-        def blend_plain_round(r):
-            blend_plain(r, 0)
-            if r + 1 < ROUNDS:
-                quantise_round(r + 1)
-            for t in range(1, ROUND_TILES):
-                blend_plain(r, t)
-
-        start_round(0)
-        regroup_weight(REASONING, 0)
-        regroup_weight(REASONING, 1)
-        for r in range(1, BIAS_LEAD + 1):
-            blend_bias(r)
-        blend_plain_round(0)
-        quantise_bank(REASONING)
-
-        for r in range(1, ROUNDS):
-            start_round(r)
-            if r + BIAS_LEAD < ROUNDS:
-                blend_bias(r + BIAS_LEAD)
-            blend_plain_round(r)
-            finish_round(r - 1)
-        finish_round(ROUNDS - 1)
+        for r in range(LAST):
+            partials = plain_half(r, [bias_plain[:]] * ROUND_TILES)
+            if r + TOKEN_LEAD < ROUNDS:
+                transpose_tokens(r + TOKEN_LEAD)
+            scaled_delta = scale_delta(r)
+            blended = reasoning_half(r, partials)
+            if r + TOKEN_LEAD < ROUNDS:
+                quantise_tokens(r + TOKEN_LEAD)
+            result = blend_pool.tile(round_shape, F32, bufs=RESULT_BUFS)
+            nc.gpsimd.tensor_tensor(out=result[:], in0=blended[:], in1=scaled_delta[:], op=ALU.add)
+            store(r, result)
+        partials = plain_half(LAST, [last_bias[:, :, t, :] for t in range(ROUND_TILES)])
+        store(LAST, reasoning_half(LAST, partials))

from contextlib import ExitStack

import concourse.mybir as mybir
from concourse.masks import make_identity

F32 = mybir.dt.float32
BF16 = mybir.dt.bfloat16
U32 = mybir.dt.uint32
U8 = mybir.dt.uint8
FP8X4 = mybir.dt.float8_e4m3fn_x4
ALU = mybir.AluOpType
ACT = mybir.ActivationFunctionType

P = 128
TOKENS = 4 * 1024
HID = 1024
FEAT = 256
PACK = 4
K_PASS = P * PACK
PASSES = HID // K_PASS
BANK = 2 * FEAT
WORDS = HID // 2
TILES = TOKENS // P
GROUP_TILES = 4
ROUND_TILES = 2
ROUNDS = TILES // ROUND_TILES
LAST = ROUNDS - 1
TOKEN_LEAD = 2
PSUM_BANKS = 8
ACC_BANKS = PSUM_BANKS - ROUND_TILES
RESULT_BUFS = 6
PLAIN, REASONING = 0, 1

FLOPS = 2 * TOKENS * HID * 4 * FEAT


def tile_reasoningmultiheadattention_pa_t_kernel(
    tc, x, reasoning_mask, Wq, bq, Wk, bk, Wqr, bqr, Wkr, bkr, out_0, out_1
):
    nc = tc.nc
    weights = (Wq, Wk, Wqr, Wkr)
    biases = (bq, bk, bqr, bkr)

    x_groups = x.rearrange("b s h -> (b s) h").rearrange(
        "(a p v) h -> a p v h", p=P, v=GROUP_TILES
    )
    gate_tiles = reasoning_mask.rearrange("b s o i -> (b s o i)").rearrange(
        "(a p v) -> p a v", p=P, v=GROUP_TILES
    )
    out_groups = [
        o.rearrange("b s n d -> (b s) (n d)").rearrange("(a p v) f -> a p v f", p=P, v=GROUP_TILES)
        for o in (out_0, out_1)
    ]

    with ExitStack() as ctx:
        keep = ctx.enter_context(tc.tile_pool(name="keep", bufs=1))
        x_pool = ctx.enter_context(tc.tile_pool(name="x_pool", bufs=ROUNDS))
        mx_pool = ctx.enter_context(tc.tile_pool(name="mx_pool", bufs=TOKEN_LEAD + 2))
        blend_pool = ctx.enter_context(tc.tile_pool(name="blend_pool", bufs=3))
        xt_pool = ctx.enter_context(tc.psum_pool(name="xt_pool", bufs=ROUND_TILES))
        acc_pool = ctx.enter_context(tc.psum_pool(name="acc_pool", bufs=ACC_BANKS))
        ctx.enter_context(tc.manual_schedule())

        bias_rows = keep.tile([P, 2, BANK], BF16)
        nc.vector.memset(bias_rows[:], 0.0)
        ones = keep.tile([P, P], BF16)
        nc.vector.memset(ones[:], 1.0)
        ident = keep.tile([P, P], F32)
        make_identity(nc, ident[:])

        x_sb = {}

        def load_tokens(r):
            a, v = divmod(r * ROUND_TILES, GROUP_TILES)
            x_round = x_pool.tile([P, ROUND_TILES, HID], BF16)
            nc.sync.dma_start(out=x_round[:], in_=x_groups[a, :, v : v + ROUND_TILES, :])
            x_sb[r] = x_round

        w_raw = {}

        def load_weights(bank):
            for side in range(2):
                raw = keep.tile([P, PASSES * PACK, FEAT], BF16, name="w_raw%d%d" % (bank, side))
                nc.sync.dma_start(
                    out=raw[:].rearrange("p (j e) n -> p j e n", e=2),
                    in_=weights[2 * bank + side].rearrange("(j p e) n -> p j e n", p=P, e=2),
                )
                w_raw[(bank, side)] = raw

        load_tokens(0)
        load_weights(PLAIN)
        for bank in (PLAIN, REASONING):
            for side in range(2):
                nc.scalar.dma_start(
                    out=bias_rows[0:1, bank, side * FEAT : (side + 1) * FEAT],
                    in_=biases[2 * bank + side].unsqueeze(0),
                )
        gate_bf = keep.tile([P, TILES], BF16)
        nc.scalar.dma_start(
            out=gate_bf[:].rearrange("p (a v) -> p a v", v=GROUP_TILES), in_=gate_tiles
        )
        load_tokens(1)
        load_weights(REASONING)
        for r in range(2, ROUNDS):
            load_tokens(r)

        grouped_of = {}
        codes_of = {}
        scales_of = {}

        def transpose_tokens(r):
            grouped = mx_pool.tile([P, ROUND_TILES * HID], BF16, align_bytes=64)
            grouped_words = grouped[:].bitcast(F32)
            x_words = x_sb[r][:].rearrange("p t h -> p (t h)").bitcast(F32)
            for t in range(ROUND_TILES):
                xt = xt_pool.tile([P, WORDS // P, P], F32)
                for j in range(WORDS // P):
                    first = t * WORDS + j * P
                    nc.tensor.transpose(
                        out=xt[:, j, :], in_=x_words[:, first : first + P], identity=ident[:]
                    )
                nc.scalar.copy(
                    out=grouped_words[:, t * WORDS : (t + 1) * WORDS].rearrange(
                        "p (c m u) -> p c m u", c=PASSES, u=2
                    ),
                    in_=xt[:].rearrange("p (c u) m -> p c m u", u=2),
                )
            grouped_of[r] = grouped

        def quantise_tokens(r):
            x_codes = mx_pool.tile([P, ROUND_TILES * PASSES * P], U32, align_bytes=64)
            x_scales = mx_pool.tile([P, ROUND_TILES * PASSES * P], U8, align_bytes=64)
            nc.vector.quantize_mx(
                out=x_codes[:].bitcast(FP8X4), scales=x_scales[:], in_=grouped_of[r][:]
            )
            codes_of[r] = x_codes
            scales_of[r] = x_scales

        w_grouped = keep.tile([P, PASSES, 2, BANK, PACK], BF16, align_bytes=64)
        w_codes = keep.tile([P, PASSES, 2, BANK], U32, align_bytes=64)
        w_scales = keep.tile([P, PASSES, 2, BANK], U8, align_bytes=64)

        def regroup_weights(bank):
            for side in range(2):
                for c in range(PASSES):
                    rows = w_raw[(bank, side)][:, c * PACK : (c + 1) * PACK, :].rearrange(
                        "p t (b i) -> p b t i", i=4
                    )
                    words = w_grouped[:, c, bank, side * FEAT : (side + 1) * FEAT, :].rearrange(
                        "p (b i) t -> p b t i", i=4
                    )
                    if bank == REASONING and c == 1:
                        nc.scalar.copy(out=words, in_=rows)
                    else:
                        nc.vector.tensor_copy(out=words, in_=rows)

        def quantise_weights(bank):
            for c in range(PASSES):
                nc.vector.quantize_mx(
                    out=w_codes[:, c, bank, :].bitcast(FP8X4),
                    scales=w_scales[:, c, bank, :],
                    in_=w_grouped[:, c, bank, :, :].rearrange("p n t -> p (n t)"),
                )

        def project(r, t, bank):
            acc = acc_pool.tile([P, BANK], F32)
            for c in range(PASSES):
                cols = slice((t * PASSES + c) * P, (t * PASSES + c + 1) * P)
                nc.tensor.matmul_mx(
                    out=acc[:],
                    lhsT=codes_of[r][:, cols].bitcast(FP8X4),
                    lhsT_scale=scales_of[r][:, cols],
                    rhs=w_codes[:, c, bank, :].bitcast(FP8X4),
                    rhs_scale=w_scales[:, c, bank, :],
                    start=(c == 0),
                    stop=(c == PASSES - 1),
                )
            return acc[:].rearrange("p (s f) -> p s f", s=2)

        bias_plain = keep.tile([P, 2, FEAT], F32)
        bias_delta = keep.tile([P, 2, FEAT], F32)
        gate = keep.tile([P, TILES], F32)
        one_minus_gate = keep.tile([P, TILES], F32)

        def plain_half(r, bias_of_tile):
            partials = []
            for t in range(ROUND_TILES):
                i = r * ROUND_TILES + t
                partial = blend_pool.tile([P, 2, FEAT], F32)
                nc.vector.scalar_tensor_tensor(
                    out=partial[:],
                    in0=project(r, t, PLAIN),
                    scalar=one_minus_gate[:, i : i + 1],
                    in1=bias_of_tile[t],
                    op0=ALU.mult,
                    op1=ALU.add,
                )
                partials.append(partial)
            return partials

        round_shape = [P, 2, ROUND_TILES, FEAT]

        def reasoning_half(r, partials):
            blended = blend_pool.tile(round_shape, F32)
            for t in range(ROUND_TILES):
                i = r * ROUND_TILES + t
                nc.vector.scalar_tensor_tensor(
                    out=blended[:, :, t, :],
                    in0=project(r, t, REASONING),
                    scalar=gate[:, i : i + 1],
                    in1=partials[t][:],
                    op0=ALU.mult,
                    op1=ALU.add,
                )
            return blended

        def scale_delta(r):
            scaled_delta = blend_pool.tile(round_shape, F32)
            for t in range(ROUND_TILES):
                i = r * ROUND_TILES + t
                nc.scalar.activation(
                    out=scaled_delta[:, :, t, :],
                    in_=bias_delta[:],
                    func=ACT.Copy,
                    scale=gate[:, i : i + 1],
                )
            return scaled_delta

        def store(r, result):
            a, v = divmod(r * ROUND_TILES, GROUP_TILES)
            for side in range(2):
                nc.sync.dma_start(
                    out=out_groups[side][a, :, v : v + ROUND_TILES, :], in_=result[:, side, :, :]
                )

        transpose_tokens(0)
        regroup_weights(PLAIN)
        quantise_tokens(0)
        quantise_weights(PLAIN)

        spread_plain = acc_pool.tile([P, BANK], F32, tag="acc")
        spread_reasoning = acc_pool.tile([P, BANK], F32, tag="acc")
        nc.tensor.matmul(
            out=spread_plain[:], lhsT=ones[:], rhs=bias_rows[:, PLAIN, :], start=True, stop=True
        )
        nc.tensor.matmul(
            out=spread_reasoning[:],
            lhsT=ones[:],
            rhs=bias_rows[:, REASONING, :],
            start=True,
            stop=True,
        )
        nc.scalar.copy(out=bias_plain[:].rearrange("p s f -> p (s f)"), in_=spread_plain[:])
        nc.scalar.copy(out=gate[:], in_=gate_bf[:])
        nc.scalar.activation(
            out=one_minus_gate[:], in_=gate_bf[:], func=ACT.Copy, bias=1.0, scale=-1.0
        )
        nc.vector.tensor_tensor(
            out=bias_delta[:].rearrange("p s f -> p (s f)"),
            in0=spread_reasoning[:],
            in1=bias_plain[:].rearrange("p s f -> p (s f)"),
            op=ALU.subtract,
        )

        transpose_tokens(1)
        regroup_weights(REASONING)
        quantise_tokens(1)
        quantise_weights(REASONING)

        last_bias = keep.tile(round_shape, F32)
        nc.gpsimd.tensor_tensor(
            out=last_bias[:],
            in0=scale_delta(LAST)[:],
            in1=bias_plain[:].unsqueeze(2).to_broadcast(round_shape),
            op=ALU.add,
        )

        for r in range(LAST):
            partials = plain_half(r, [bias_plain[:]] * ROUND_TILES)
            if r + TOKEN_LEAD < ROUNDS:
                transpose_tokens(r + TOKEN_LEAD)
            scaled_delta = scale_delta(r)
            blended = reasoning_half(r, partials)
            if r + TOKEN_LEAD < ROUNDS:
                quantise_tokens(r + TOKEN_LEAD)
            result = blend_pool.tile(round_shape, F32, bufs=RESULT_BUFS)
            nc.gpsimd.tensor_tensor(out=result[:], in0=blended[:], in1=scaled_delta[:], op=ALU.add)
            store(r, result)
        partials = plain_half(LAST, [last_bias[:, :, t, :] for t in range(ROUND_TILES)])
        store(LAST, reasoning_half(LAST, partials))
